import numpy as np
import ml_dtypes


def mxq(x, axis, fmt="e4m3"):
    dtype, down = {"e4m3": (ml_dtypes.float8_e4m3fn, 7), "e5m2": (ml_dtypes.float8_e5m2, 14)}[fmt]
    v = np.moveaxis(np.asarray(x, np.float32).astype(ml_dtypes.bfloat16).astype(np.float64), axis, -1)
    blocks = v.reshape(v.shape[:-1] + (-1, 32))
    amax = np.abs(blocks).max(-1, keepdims=True)
    byte = np.maximum(np.where(amax > 0, np.frexp(amax)[1] - 1 + 127, 0) - down, 1)
    scale = np.exp2(byte - 127.0)
    codes = (blocks / scale).astype(np.float32).astype(dtype).astype(np.float64)
    return np.moveaxis((codes * scale).reshape(v.shape), -1, axis)


WIDE = False


def mx_kscale(k):
    if not WIDE:
        return np.ones(k)
    levels = np.array([10, -10, 5, -5, 0])
    if k % 512:
        return np.exp2(np.random.permutation(np.resize(levels, k // 32))).repeat(32)
    a = np.empty((k // 512, 16))
    for p in range(k // 512):
        a[p, :8] = np.random.permutation(np.resize(levels, 8))
        for g in range(8):
            far = levels[np.abs(levels - a[p, g]) >= 10]
            a[p, g + 8] = far[np.random.randint(len(far))]
    return np.exp2(a.ravel()).repeat(32)


BF16 = ml_dtypes.bfloat16


def bf(x):
    return np.asarray(x, np.float32).astype(BF16)


def f64(x):
    return np.asarray(x).astype(np.float64)


T, D, E = 1024, 6144, 768


def setup_inputs():
    s = mx_kscale(D)
    return {"hidden_states": bf(np.random.standard_normal((T, D)) * s),
            "weight": bf(np.random.standard_normal((E, D)) * 1.0 / np.sqrt(D) / s[None, :])}


def reference(hidden_states, weight):
    logits = mxq(f64(hidden_states), 1, "e4m3") @ mxq(f64(weight), 1, "e4m3").T
    return logits

@@ -1,0 +1,276 @@
+from contextlib import ExitStack
+
+import concourse.mybir as mybir
+from concourse.masks import make_identity
+
+F32 = mybir.dt.float32
+BF16 = mybir.dt.bfloat16
+U32 = mybir.dt.uint32
+U8 = mybir.dt.uint8
+FP8X4 = mybir.dt.float8_e4m3fn_x4
+
+P = 128
+T_ROWS, D, E = 1024, 6144, 768
+N_PASS = 12
+FLOPS = 2 * T_ROWS * D * E
+NR = 6
+
+
+def tile_longcatrouter_kernel(tc, hidden_states, weight, out):
+    nc = tc.nc
+    hid = hidden_states.rearrange("(i p) k -> p i k", p=P)
+    wgt = weight.rearrange("(a p) k -> p a k", p=P)
+
+    with ExitStack() as ctx:
+        const = ctx.enter_context(tc.tile_pool(name="const", bufs=1))
+        keep = ctx.enter_context(tc.tile_pool(name="keep", bufs=1))
+        rawp = ctx.enter_context(tc.tile_pool(name="rawp", bufs=NR))
+        grp = ctx.enter_context(tc.tile_pool(name="grp", bufs=6))
+        osp = ctx.enter_context(tc.tile_pool(name="osp", bufs=4))
+        psum = ctx.enter_context(tc.psum_pool(name="psum", bufs=1))
+        ctx.enter_context(tc.manual_schedule())
+
+        raw = {}
+        st = {"next": 0, "raw_free": NR, "bank": 0}
+
+        def new_raw(kind, c):
+            width = 4096 if kind in ("w", "h") else 6144
+            t = rawp.tile([P, width], BF16, name="raw", tag="raw")
+            raw[(kind, c)] = t
+            return t
+
+        def source(kind, k0, k1):
+            if kind == "w":
+                return wgt[:, 0:4, k0:k1]
+            return hid[:, 0:4, k0:k1]
+
+        w0 = new_raw("w", 0)
+        h0 = new_raw("h", 0)
+        st["raw_free"] -= 2
+        for pl in range(2):
+            for kind, t in (("w", w0), ("h", h0)):
+                nc.sync.dma_start(
+                    out=t[:].rearrange("p (a k) -> p a k", a=4)[:, :, 512 * pl : 512 * (pl + 1)],
+                    in_=source(kind, 512 * pl, 512 * (pl + 1)),
+                )
+
+        loads = []
+        for c in range(1, 6):
+            loads.extend([("w", c), ("h", c)])
+        loads.extend([("x", 0), ("x", 1), ("g", 4), ("g", 5), ("g", 6), ("g", 7)])
+
+        def pump():
+            while st["next"] < len(loads):
+                kind, c = loads[st["next"]]
+                if st["raw_free"] == 0:
+                    break
+                st["raw_free"] -= 1
+                st["next"] += 1
+                t = new_raw(kind, c)
+                if kind == "x":
+                    nc.sync.dma_start(
+                        out=t[:].rearrange("p (a k) -> p a k", a=2),
+                        in_=wgt[:, 4:6, 3072 * c : 3072 * (c + 1)],
+                    )
+                elif kind == "g":
+                    nc.sync.dma_start(out=t[:], in_=hid[:, c, :])
+                else:
+                    nc.sync.dma_start(
+                        out=t[:].rearrange("p (a k) -> p a k", a=4),
+                        in_=source(kind, 1024 * c, 1024 * (c + 1)),
+                    )
+
+        pump()
+
+        ident = const.tile([P, P], F32)
+        make_identity(nc, ident[:])
+
+        cA = keep.tile([P, N_PASS * 1024], U32, align_bytes=64)
+        sA = keep.tile([P, N_PASS * 1024], U8, align_bytes=64)
+        cH = keep.tile([P, N_PASS * 512], U32, align_bytes=64)
+        sH = keep.tile([P, N_PASS * 512], U8, align_bytes=64)
+        cX = keep.tile([P, N_PASS * 256], U32, align_bytes=64)
+        sX = keep.tile([P, N_PASS * 256], U8, align_bytes=64)
+
+        def bank(words, offs, on_vector, gt, half):
+            b = st["bank"]
+            st["bank"] = (b + 1) % 4
+            bk = psum.tile([P, 512], F32, name="tb%d" % b, tag="tb%d" % b)
+            for a in range(2):
+                for u in range(2):
+                    j = 2 * a + u
+                    nc.tensor.transpose(
+                        bk[:, 128 * j : 128 * (j + 1)],
+                        words[:, offs[a] + u : offs[a] + 256 : 2],
+                        ident[:],
+                    )
+            dst = gt[:].bitcast(F32)[:, 512 * half : 512 * (half + 1)].rearrange(
+                "p (a r u) -> p a r u", a=2, u=2
+            )
+            src = bk[:].rearrange("p (a u r) -> p a r u", a=2, u=2)
+            if on_vector:
+                nc.vector.tensor_copy(out=dst, in_=src)
+            else:
+                nc.scalar.copy(out=dst, in_=src)
+
+        def new_group():
+            gt = grp.tile([P, 2048], BF16, name="grouped", tag="grouped", align_bytes=64)
+            return gt
+
+        def quant(gt, codes, scales, c0):
+            nc.vector.quantize_mx(
+                out=codes[:, c0 : c0 + 512].bitcast(FP8X4),
+                scales=scales[:, c0 : c0 + 512],
+                in_=gt[:],
+            )
+
+        def t_four(kind, c, pl, eng):
+            words = raw[(kind, c)][:].bitcast(F32)
+            gt = new_group()
+            bank(words, (256 * pl, 512 + 256 * pl), eng[0], gt, 0)
+            bank(words, (1024 + 256 * pl, 1536 + 256 * pl), eng[1], gt, 1)
+            return gt
+
+        def dest(kind, g):
+            if kind == "w":
+                return (cA, sA, 1024 * g)
+            return (cA, sA, 1024 * g + 512)
+
+        def t8(kind, c, pl):
+            gt = t_four(kind, c, pl, (False, True))
+            quant(gt, *dest(kind, 2 * c + pl))
+
+        def t16(kind, c):
+            g0 = t_four(kind, c, 0, (False, False))
+            g1 = t_four(kind, c, 1, (False, True))
+            quant(g0, *dest(kind, 2 * c))
+            quant(g1, *dest(kind, 2 * c + 1))
+            st["raw_free"] += 1
+            pump()
+
+        def t24(words, offs, codes, scales, c0):
+            g0 = new_group()
+            bank(words, offs[0], False, g0, 0)
+            bank(words, offs[1], False, g0, 1)
+            g1 = new_group()
+            bank(words, offs[2], True, g1, 0)
+            quant(g0, codes, scales, c0[0])
+            bank(words, offs[3], False, g1, 1)
+            g2 = new_group()
+            bank(words, offs[4], False, g2, 0)
+            bank(words, offs[5], True, g2, 1)
+            quant(g1, codes, scales, c0[1])
+            quant(g2, codes, scales, c0[2])
+            st["raw_free"] += 1
+            pump()
+
+        def tx(half):
+            words = raw[("x", half)][:].bitcast(F32)
+            offs = [(256 * pl, 1536 + 256 * pl) for pl in range(6)]
+            t24(words, offs, cX, sX, [256 * (6 * half + 2 * q) for q in range(3)])
+
+        def tg(i):
+            words = raw[("g", i)][:].bitcast(F32)
+            offs = [(256 * (2 * b), 256 * (2 * b + 1)) for b in range(6)]
+            t24(words, offs, cH, sH, [1536 * (i - 4) + 512 * m for m in range(3)])
+
+        def mx(acc_ap, lc, ls, l0, rc, rs, r0, n, start, stop):
+            nc.tensor.matmul_mx(
+                out=acc_ap,
+                lhsT=lc[:, l0 : l0 + P].bitcast(FP8X4),
+                lhsT_scale=ls[:, l0 : l0 + P],
+                rhs=rc[:, r0 : r0 + n].bitcast(FP8X4),
+                rhs_scale=rs[:, r0 : r0 + n],
+                start=start,
+                stop=stop,
+            )
+
+        acc = {}
+
+        def open_acc():
+            for i in range(4):
+                acc[i] = psum.tile([P, 512], F32, name="acc%d" % i, tag="acc%d" % i)
+
+        def drain_acc(first_tile):
+            for i in range(4):
+                ot = osp.tile([P, 512], F32, name="ost", tag="ost")
+                if i % 2 == 0:
+                    nc.vector.tensor_copy(out=ot[:], in_=acc[i][:])
+                else:
+                    nc.scalar.copy(out=ot[:], in_=acc[i][:])
+                r0 = P * (first_tile + i)
+                nc.sync.dma_start(out=out[r0 : r0 + P, 0:512], in_=ot[:])
+
+        def m_first(g):
+            if g == 0:
+                open_acc()
+            for i in range(4):
+                mx(acc[i][:], cA, sA, 1024 * g + 512 + P * i, cA, sA, 1024 * g, 512,
+                   g == 0, g == N_PASS - 1)
+            if g == N_PASS - 1:
+                drain_acc(0)
+
+        def store_small(src_ap, i, on_vector):
+            o3 = osp.tile([P, 256], F32, name="o3", tag="o3")
+            if on_vector:
+                nc.vector.tensor_copy(out=o3[:], in_=src_ap)
+            else:
+                nc.scalar.copy(out=o3[:], in_=src_ap)
+            nc.sync.dma_start(out=out[P * i : P * (i + 1), 512:768], in_=o3[:])
+
+        def r3a(half):
+            if half == 0:
+                open_acc()
+            for g in range(6 * half, 6 * half + 6):
+                for i in range(4):
+                    mx(acc[i][:, 0:256], cA, sA, 1024 * g + 512 + P * i, cX, sX, 256 * g, 256,
+                       g == 0, g == N_PASS - 1)
+            if half == 1:
+                for i in range(4):
+                    store_small(acc[i][:, 0:256], i, i % 2 == 0)
+
+        def mc(i):
+            j = 2 * (i % 2)
+            pa = psum.tile([P, 512], F32, name="mca%d" % i, tag="acc%d" % j)
+            pb = psum.tile([P, 512], F32, name="mcb%d" % i, tag="acc%d" % (j + 1))
+            for g in range(N_PASS):
+                mx(pa[:], cH, sH, 1536 * (i - 4) + P * g, cA, sA, 1024 * g, 512,
+                   g == 0, g == N_PASS - 1)
+            ot = osp.tile([P, 512], F32, name="ost", tag="ost")
+            nc.vector.tensor_copy(out=ot[:], in_=pa[:])
+            nc.sync.dma_start(out=out[P * i : P * (i + 1), 0:512], in_=ot[:])
+            for g in range(N_PASS):
+                mx(pb[:, 0:256], cH, sH, 1536 * (i - 4) + P * g, cX, sX, 256 * g, 256,
+                   g == 0, g == N_PASS - 1)
+            store_small(pb[:, 0:256], i, False)
+
+        t8("w", 0, 0)
+        t8("h", 0, 0)
+        t8("w", 0, 1)
+        m_first(0)
+        t8("h", 0, 1)
+        st["raw_free"] += 2
+        pump()
+        t16("w", 1)
+        m_first(1)
+        t16("h", 1)
+        for c in range(2, 6):
+            t16("w", c)
+            m_first(2 * c - 2)
+            t16("h", c)
+            m_first(2 * c - 1)
+
+        tx(0)
+        m_first(10)
+        tx(1)
+        m_first(11)
+        tg(4)
+        r3a(0)
+        tg(5)
+        r3a(1)
+        tg(6)
+        mc(4)
+        tg(7)
+        mc(5)
+        mc(6)
+        mc(7)

@@ -25,13 +25,14 @@ def tile_longcatrouter_kernel(tc, hidden_states, weight, out):
         const = ctx.enter_context(tc.tile_pool(name="const", bufs=1))
         keep = ctx.enter_context(tc.tile_pool(name="keep", bufs=1))
         rawp = ctx.enter_context(tc.tile_pool(name="rawp", bufs=NR))
-        grp = ctx.enter_context(tc.tile_pool(name="grp", bufs=6))
+        sortp = ctx.enter_context(tc.tile_pool(name="sortp", bufs=6))
+        grp = ctx.enter_context(tc.tile_pool(name="grp", bufs=4))
         osp = ctx.enter_context(tc.tile_pool(name="osp", bufs=4))
         psum = ctx.enter_context(tc.psum_pool(name="psum", bufs=1))
         ctx.enter_context(tc.manual_schedule())
 
         raw = {}
-        st = {"next": 0, "raw_free": NR, "bank": 0}
+        st = {"next": 0, "raw_free": NR}
 
         def new_raw(kind, c):
             width = 4096 if kind in ("w", "h") else 6144
@@ -57,7 +58,7 @@ def tile_longcatrouter_kernel(tc, hidden_states, weight, out):
         loads = []
         for c in range(1, 6):
             loads.extend([("w", c), ("h", c)])
-        loads.extend([("x", 0), ("x", 1), ("g", 4), ("g", 5), ("g", 6), ("g", 7)])
+        loads.extend([("g", 4), ("g", 5), ("g", 6), ("g", 7), ("x", 0), ("x", 1)])
 
         def pump():
             while st["next"] < len(loads):
@@ -92,185 +93,178 @@ def tile_longcatrouter_kernel(tc, hidden_states, weight, out):
         cX = keep.tile([P, N_PASS * 256], U32, align_bytes=64)
         sX = keep.tile([P, N_PASS * 256], U8, align_bytes=64)
 
-        def bank(words, offs, on_vector, gt, half):
-            b = st["bank"]
-            st["bank"] = (b + 1) % 4
-            bk = psum.tile([P, 512], F32, name="tb%d" % b, tag="tb%d" % b)
-            for a in range(2):
-                for u in range(2):
-                    j = 2 * a + u
-                    nc.tensor.transpose(
-                        bk[:, 128 * j : 128 * (j + 1)],
-                        words[:, offs[a] + u : offs[a] + 256 : 2],
-                        ident[:],
-                    )
-            dst = gt[:].bitcast(F32)[:, 512 * half : 512 * (half + 1)].rearrange(
-                "p (a r u) -> p a r u", a=2, u=2
+        ROWS = {"w": 4, "h": 4, "x": 2, "g": 1}
+        PARTS = {"w": 2, "h": 2, "x": 3, "g": 3}
+        sorted_words = {}
+        grouped = {}
+
+        def batch_words(b):
+            kind, c, part = b
+            rows = ROWS[kind]
+            span = 1024 // rows
+            words = raw[(kind, c)][:].bitcast(F32).rearrange("p (a k) -> p a k", a=rows)
+            return words[:, :, span * part : span * (part + 1)]
+
+        def sort(b):
+            kind, c, part = b
+            rows = ROWS[kind]
+            s = sortp.tile([P, 1024], F32, name="sorted", tag="sorted")
+            nc.vector.tensor_copy(
+                out=s[:].rearrange("p (a u q) -> p a u q", a=rows, u=2),
+                in_=batch_words(b).rearrange("p a (q u) -> p a u q", u=2),
             )
-            src = bk[:].rearrange("p (a u r) -> p a r u", a=2, u=2)
-            if on_vector:
-                nc.vector.tensor_copy(out=dst, in_=src)
-            else:
-                nc.scalar.copy(out=dst, in_=src)
+            sorted_words[b] = s
+            if part == PARTS[kind] - 1:
+                st["raw_free"] += 1
+                pump()
 
-        def new_group():
+        def transpose_batch(b, first_bank):
+            kind, c, part = b
+            rows = ROWS[kind]
+            span = 1024 // rows
             gt = grp.tile([P, 2048], BF16, name="grouped", tag="grouped", align_bytes=64)
-            return gt
+            for half in range(2):
+                n = first_bank + half
+                bk = psum.tile([P, 512], F32, name="tb%d" % n, tag="tb%d" % n)
+                for s in range(2):
+                    slot = 2 * half + s
+                    a = slot % rows
+                    g = slot // rows
+                    for u in range(2):
+                        if b in sorted_words:
+                            k0 = span * a + span // 2 * u + P * g
+                            src = sorted_words[b][:, k0 : k0 + P]
+                        else:
+                            src = batch_words(b)[:, a, 256 * g + u : 256 * (g + 1) : 2]
+                        j = 2 * s + u
+                        nc.tensor.transpose(bk[:, P * j : P * (j + 1)], src, ident[:])
+                nc.scalar.copy(
+                    out=gt[:].bitcast(F32)[:, 512 * half : 512 * (half + 1)].rearrange(
+                        "p (a r u) -> p a r u", a=2, u=2
+                    ),
+                    in_=bk[:].rearrange("p (a u r) -> p a r u", a=2, u=2),
+                )
+            grouped[b] = gt
 
-        def quant(gt, codes, scales, c0):
+        def quant(b):
+            kind, c, part = b
+            if kind == "w":
+                codes, scales, c0 = cA, sA, 1024 * (2 * c + part)
+            elif kind == "h":
+                codes, scales, c0 = cA, sA, 1024 * (2 * c + part) + 512
+            elif kind == "x":
+                codes, scales, c0 = cX, sX, 512 * (3 * c + part)
+            else:
+                codes, scales, c0 = cH, sH, 1536 * (c - 4) + 512 * part
             nc.vector.quantize_mx(
                 out=codes[:, c0 : c0 + 512].bitcast(FP8X4),
                 scales=scales[:, c0 : c0 + 512],
-                in_=gt[:],
+                in_=grouped[b][:],
             )
 
-        def t_four(kind, c, pl, eng):
-            words = raw[(kind, c)][:].bitcast(F32)
-            gt = new_group()
-            bank(words, (256 * pl, 512 + 256 * pl), eng[0], gt, 0)
-            bank(words, (1024 + 256 * pl, 1536 + 256 * pl), eng[1], gt, 1)
-            return gt
-
-        def dest(kind, g):
-            if kind == "w":
-                return (cA, sA, 1024 * g)
-            return (cA, sA, 1024 * g + 512)
-
-        def t8(kind, c, pl):
-            gt = t_four(kind, c, pl, (False, True))
-            quant(gt, *dest(kind, 2 * c + pl))
-
-        def t16(kind, c):
-            g0 = t_four(kind, c, 0, (False, False))
-            g1 = t_four(kind, c, 1, (False, True))
-            quant(g0, *dest(kind, 2 * c))
-            quant(g1, *dest(kind, 2 * c + 1))
-            st["raw_free"] += 1
-            pump()
-
-        def t24(words, offs, codes, scales, c0):
-            g0 = new_group()
-            bank(words, offs[0], False, g0, 0)
-            bank(words, offs[1], False, g0, 1)
-            g1 = new_group()
-            bank(words, offs[2], True, g1, 0)
-            quant(g0, codes, scales, c0[0])
-            bank(words, offs[3], False, g1, 1)
-            g2 = new_group()
-            bank(words, offs[4], False, g2, 0)
-            bank(words, offs[5], True, g2, 1)
-            quant(g1, codes, scales, c0[1])
-            quant(g2, codes, scales, c0[2])
-            st["raw_free"] += 1
-            pump()
-
-        def tx(half):
-            words = raw[("x", half)][:].bitcast(F32)
-            offs = [(256 * pl, 1536 + 256 * pl) for pl in range(6)]
-            t24(words, offs, cX, sX, [256 * (6 * half + 2 * q) for q in range(3)])
-
-        def tg(i):
-            words = raw[("g", i)][:].bitcast(F32)
-            offs = [(256 * (2 * b), 256 * (2 * b + 1)) for b in range(6)]
-            t24(words, offs, cH, sH, [1536 * (i - 4) + 512 * m for m in range(3)])
-
-        def mx(acc_ap, lc, ls, l0, rc, rs, r0, n, start, stop):
+        def mx(acc_ap, lc, ls, l0, rc, rs, r0, n, g):
             nc.tensor.matmul_mx(
                 out=acc_ap,
                 lhsT=lc[:, l0 : l0 + P].bitcast(FP8X4),
                 lhsT_scale=ls[:, l0 : l0 + P],
                 rhs=rc[:, r0 : r0 + n].bitcast(FP8X4),
                 rhs_scale=rs[:, r0 : r0 + n],
-                start=start,
-                stop=stop,
+                start=g == 0,
+                stop=g == N_PASS - 1,
             )
 
         acc = {}
 
-        def open_acc():
-            for i in range(4):
-                acc[i] = psum.tile([P, 512], F32, name="acc%d" % i, tag="acc%d" % i)
+        def open_acc(j):
+            acc[j] = psum.tile([P, 512], F32, name="acc%d" % j, tag="acc%d" % j)
 
-        def drain_acc(first_tile):
-            for i in range(4):
-                ot = osp.tile([P, 512], F32, name="ost", tag="ost")
-                if i % 2 == 0:
-                    nc.vector.tensor_copy(out=ot[:], in_=acc[i][:])
-                else:
-                    nc.scalar.copy(out=ot[:], in_=acc[i][:])
-                r0 = P * (first_tile + i)
-                nc.sync.dma_start(out=out[r0 : r0 + P, 0:512], in_=ot[:])
-
-        def m_first(g):
-            if g == 0:
-                open_acc()
-            for i in range(4):
-                mx(acc[i][:], cA, sA, 1024 * g + 512 + P * i, cA, sA, 1024 * g, 512,
-                   g == 0, g == N_PASS - 1)
-            if g == N_PASS - 1:
-                drain_acc(0)
-
-        def store_small(src_ap, i, on_vector):
-            o3 = osp.tile([P, 256], F32, name="o3", tag="o3")
+        def drain(j, i, n, on_vector):
+            ot = osp.tile([P, n], F32, name="ot%d" % n, tag="ot%d" % n)
             if on_vector:
-                nc.vector.tensor_copy(out=o3[:], in_=src_ap)
+                nc.vector.tensor_copy(out=ot[:], in_=acc[j][:, 0:n])
             else:
-                nc.scalar.copy(out=o3[:], in_=src_ap)
-            nc.sync.dma_start(out=out[P * i : P * (i + 1), 512:768], in_=o3[:])
+                nc.scalar.copy(out=ot[:], in_=acc[j][:, 0:n])
+            e0 = 0 if n == 512 else 512
+            nc.sync.dma_start(out=out[P * i : P * (i + 1), e0 : e0 + n], in_=ot[:])
 
-        def r3a(half):
-            if half == 0:
-                open_acc()
-            for g in range(6 * half, 6 * half + 6):
-                for i in range(4):
-                    mx(acc[i][:, 0:256], cA, sA, 1024 * g + 512 + P * i, cX, sX, 256 * g, 256,
-                       g == 0, g == N_PASS - 1)
-            if half == 1:
-                for i in range(4):
-                    store_small(acc[i][:, 0:256], i, i % 2 == 0)
+        late = []
 
-        def mc(i):
-            j = 2 * (i % 2)
-            pa = psum.tile([P, 512], F32, name="mca%d" % i, tag="acc%d" % j)
-            pb = psum.tile([P, 512], F32, name="mcb%d" % i, tag="acc%d" % (j + 1))
+        def first(g):
+            for i in range(4):
+                if g == 0:
+                    open_acc(i)
+                mx(acc[i][:], cA, sA, 1024 * g + 512 + P * i, cA, sA, 1024 * g, 512, g)
+                if g == N_PASS - 1:
+                    if i % 2 == 0:
+                        drain(i, i, 512, False)
+                    else:
+                        late.append(i)
+
+        def token_batch(b):
+            kind, i, part = b
+            if part == 0:
+                open_acc(i - 4)
+            for g in range(4 * part, 4 * part + 4):
+                mx(acc[i - 4][:], cH, sH, 1536 * (i - 4) + P * g, cA, sA, 1024 * g, 512, g)
+            if part == 2:
+                drain(i - 4, i, 512, False)
+
+        def last_low(q):
+            for i in range(4):
+                if q == 0:
+                    open_acc(i)
+                for g in range(4 * q, 4 * q + 4):
+                    mx(acc[i][:, 0:256], cA, sA, 1024 * g + 512 + P * i, cX, sX, 256 * g, 256, g)
+                if q == 2:
+                    drain(i, i, 256, i % 2 == 0)
+
+        def last_high(i):
+            open_acc(i - 4)
             for g in range(N_PASS):
-                mx(pa[:], cH, sH, 1536 * (i - 4) + P * g, cA, sA, 1024 * g, 512,
-                   g == 0, g == N_PASS - 1)
-            ot = osp.tile([P, 512], F32, name="ost", tag="ost")
-            nc.vector.tensor_copy(out=ot[:], in_=pa[:])
-            nc.sync.dma_start(out=out[P * i : P * (i + 1), 0:512], in_=ot[:])
-            for g in range(N_PASS):
-                mx(pb[:, 0:256], cH, sH, 1536 * (i - 4) + P * g, cX, sX, 256 * g, 256,
-                   g == 0, g == N_PASS - 1)
-            store_small(pb[:, 0:256], i, False)
+                mx(acc[i - 4][:, 0:256], cH, sH, 1536 * (i - 4) + P * g, cX, sX, 256 * g, 256, g)
+            drain(i - 4, i, 256, i % 2 == 0)
 
-        t8("w", 0, 0)
-        t8("h", 0, 0)
-        t8("w", 0, 1)
-        m_first(0)
-        t8("h", 0, 1)
-        st["raw_free"] += 2
-        pump()
-        t16("w", 1)
-        m_first(1)
-        t16("h", 1)
-        for c in range(2, 6):
-            t16("w", c)
-            m_first(2 * c - 2)
-            t16("h", c)
-            m_first(2 * c - 1)
+        runs = [(("w", 0, 0), ("h", 0, 0)), (("w", 0, 1), ("h", 0, 1))]
+        for c in range(1, 6):
+            for kind in ("w", "h"):
+                runs.append(((kind, c, 0), (kind, c, 1)))
+        parts = [("g", i, part) for i in range(4, 8) for part in range(3)]
+        parts += [("x", half, part) for half in range(2) for part in range(3)]
+        runs += [(parts[2 * n], parts[2 * n + 1]) for n in range(9)]
 
-        tx(0)
-        m_first(10)
-        tx(1)
-        m_first(11)
-        tg(4)
-        r3a(0)
-        tg(5)
-        r3a(1)
-        tg(6)
-        mc(4)
-        tg(7)
-        mc(5)
-        mc(6)
-        mc(7)
+        def multiply(n):
+            if n in (1, 2):
+                first(n - 1)
+            elif 4 <= n <= 13:
+                first(n - 2)
+            elif 14 <= n <= 19:
+                for b in runs[n - 2]:
+                    token_batch(b)
+            elif n == 20:
+                last_low(0)
+                last_low(1)
+
+        todo = [b for run in runs[1:] for b in run]
+
+        def sort_to(count):
+            while todo and len(sorted_words) < count:
+                sort(todo.pop(0))
+
+        for n in range(len(runs)):
+            ahead = 1 if n < 4 else 2
+            one, two = runs[n]
+            transpose_batch(one, 0)
+            transpose_batch(two, 2)
+            if n > 0:
+                quant(runs[n - 1][1])
+            while late:
+                j = late.pop(0)
+                drain(j, j, 512, True)
+            sort_to(2 * (n + ahead) - 1)
+            quant(one)
+            sort_to(2 * (n + ahead))
+            multiply(n)
+        quant(runs[-1][1])
+        last_low(2)
+        for i in range(4, 8):
+            last_high(i)

@@ -13,7 +13,7 @@ P = 128
 T_ROWS, D, E = 1024, 6144, 768
 N_PASS = 12
 FLOPS = 2 * T_ROWS * D * E
-NR = 6
+NR = 5
 
 
 def tile_longcatrouter_kernel(tc, hidden_states, weight, out):
@@ -23,6 +23,7 @@ def tile_longcatrouter_kernel(tc, hidden_states, weight, out):
 
     with ExitStack() as ctx:
         const = ctx.enter_context(tc.tile_pool(name="const", bufs=1))
+        headp = ctx.enter_context(tc.tile_pool(name="headp", bufs=1))
         keep = ctx.enter_context(tc.tile_pool(name="keep", bufs=1))
         rawp = ctx.enter_context(tc.tile_pool(name="rawp", bufs=NR))
         sortp = ctx.enter_context(tc.tile_pool(name="sortp", bufs=6))
@@ -32,11 +33,11 @@ def tile_longcatrouter_kernel(tc, hidden_states, weight, out):
         ctx.enter_context(tc.manual_schedule())
 
         raw = {}
-        st = {"next": 0, "raw_free": NR}
+        st = {"next": 0, "raw_free": NR, "bank": 0, "banks": 4}
 
         def new_raw(kind, c):
             width = 4096 if kind in ("w", "h") else 6144
-            t = rawp.tile([P, width], BF16, name="raw", tag="raw")
+            t = rawp.tile([P, width], BF16, name="raw", tag="raw", align_bytes=64)
             raw[(kind, c)] = t
             return t
 
@@ -45,20 +46,25 @@ def tile_longcatrouter_kernel(tc, hidden_states, weight, out):
                 return wgt[:, 0:4, k0:k1]
             return hid[:, 0:4, k0:k1]
 
-        w0 = new_raw("w", 0)
-        h0 = new_raw("h", 0)
-        st["raw_free"] -= 2
-        for pl in range(2):
-            for kind, t in (("w", w0), ("h", h0)):
+        def load_first(kind, pl, pairs):
+            t = headp.tile([P, 2048], BF16, name="head_%s%d" % (kind, pl), tag="head_%s%d" % (kind, pl))
+            raw[(kind, 0, pl)] = t
+            src = wgt if kind == "w" else hid
+            for a0, a1 in pairs:
                 nc.sync.dma_start(
-                    out=t[:].rearrange("p (a k) -> p a k", a=4)[:, :, 512 * pl : 512 * (pl + 1)],
-                    in_=source(kind, 512 * pl, 512 * (pl + 1)),
+                    out=t[:].rearrange("p (a k) -> p a k", a=4)[:, a0:a1, :],
+                    in_=src[:, a0:a1, 512 * pl : 512 * (pl + 1)],
                 )
+
+        load_first("w", 0, ((0, 2), (2, 4)))
+        load_first("h", 0, ((0, 2), (2, 4)))
+        load_first("w", 1, ((0, 4),))
+        load_first("h", 1, ((0, 4),))
 
         loads = []
         for c in range(1, 6):
             loads.extend([("w", c), ("h", c)])
-        loads.extend([("g", 4), ("g", 5), ("g", 6), ("g", 7), ("x", 0), ("x", 1)])
+        loads.extend([("g", 4), ("g", 5), ("x", 0), ("x", 1)])
 
         def pump():
             while st["next"] < len(loads):
@@ -83,6 +89,15 @@ def tile_longcatrouter_kernel(tc, hidden_states, weight, out):
 
         pump()
 
+        def load_turned(i, r, q):
+            if (r, q) == (0, 0):
+                new_raw("v", i)
+            t0 = P * i + 32 * r
+            nc.sync.dma_start(
+                out=raw[("v", i)][32 * q : 32 * (q + 1), 1536 * r : 1536 * (r + 1)].rearrange("p (g k) -> p g k", k=P),
+                in_=hidden_states[t0 : t0 + 32, :].rearrange("p (g k) -> p g k", k=512)[:, :, P * q : P * (q + 1)],
+            )
+
         ident = const.tile([P, P], F32)
         make_identity(nc, ident[:])
 
@@ -102,30 +117,33 @@ def tile_longcatrouter_kernel(tc, hidden_states, weight, out):
             kind, c, part = b
             rows = ROWS[kind]
             span = 1024 // rows
+            if (kind, c, part) in raw:
+                return raw[(kind, c, part)][:].bitcast(F32).rearrange("p (a k) -> p a k", a=rows)
             words = raw[(kind, c)][:].bitcast(F32).rearrange("p (a k) -> p a k", a=rows)
             return words[:, :, span * part : span * (part + 1)]
 
         def sort(b):
             kind, c, part = b
             rows = ROWS[kind]
-            s = sortp.tile([P, 1024], F32, name="sorted", tag="sorted")
+            s = sortp.tile([P, 1024], F32, name="sorted", tag="sorted", align_bytes=64)
             nc.vector.tensor_copy(
                 out=s[:].rearrange("p (a u q) -> p a u q", a=rows, u=2),
                 in_=batch_words(b).rearrange("p a (q u) -> p a u q", u=2),
             )
             sorted_words[b] = s
-            if part == PARTS[kind] - 1:
+            if (kind, c) in raw and part == PARTS[kind] - 1:
                 st["raw_free"] += 1
                 pump()
 
-        def transpose_batch(b, first_bank):
+        def transpose_batch(b, share):
             kind, c, part = b
             rows = ROWS[kind]
             span = 1024 // rows
             gt = grp.tile([P, 2048], BF16, name="grouped", tag="grouped", align_bytes=64)
             for half in range(2):
-                n = first_bank + half
-                bk = psum.tile([P, 512], F32, name="tb%d" % n, tag="tb%d" % n)
+                n = st["bank"]
+                st["bank"] = (n + 1) % st["banks"]
+                bk = psum.tile([P, 512], F32, name="b%d" % n, tag="b%d" % n)
                 for s in range(2):
                     slot = 2 * half + s
                     a = slot % rows
@@ -138,13 +156,39 @@ def tile_longcatrouter_kernel(tc, hidden_states, weight, out):
                             src = batch_words(b)[:, a, 256 * g + u : 256 * (g + 1) : 2]
                         j = 2 * s + u
                         nc.tensor.transpose(bk[:, P * j : P * (j + 1)], src, ident[:])
-                nc.scalar.copy(
-                    out=gt[:].bitcast(F32)[:, 512 * half : 512 * (half + 1)].rearrange(
-                        "p (a r u) -> p a r u", a=2, u=2
-                    ),
-                    in_=bk[:].rearrange("p (a u r) -> p a r u", a=2, u=2),
+                dst = gt[:].bitcast(F32)[:, 512 * half : 512 * (half + 1)].rearrange(
+                    "p (a r u) -> p a r u", a=2, u=2
                 )
+                src = bk[:].rearrange("p (a u r) -> p a r u", a=2, u=2)
+                if share and half == 1:
+                    nc.vector.tensor_copy(out=dst, in_=src)
+                else:
+                    nc.scalar.copy(out=dst, in_=src)
             grouped[b] = gt
+
+        turned = {}
+
+        def turn_rows(i, r):
+            s = sortp.tile([P, 768], F32, name="sorted", tag="sorted", align_bytes=64)
+            nc.vector.tensor_copy(
+                out=s[:].rearrange("p (u q) -> p u q", u=2),
+                in_=raw[("v", i)][:].bitcast(F32)[:, 768 * r : 768 * (r + 1)].rearrange("p (q u) -> p u q", u=2),
+            )
+            return s
+
+        def turn_blocks(i, r, s):
+            nc.vector.transpose(turned[i][:, 768 * r : 768 * (r + 1)], s[:])
+
+        def gather_turned(i, m):
+            gt = grp.tile([P, 2048], BF16, name="grouped", tag="grouped", align_bytes=64)
+            for r in range(4):
+                nc.scalar.copy(
+                    out=gt[:].bitcast(F32).rearrange("p (g r t u) -> p r g t u", g=4, r=4, u=2)[:, r],
+                    in_=turned[i][:, 768 * r : 768 * (r + 1)].rearrange("p (u g t) -> p g t u", u=2, t=32)[
+                        :, 4 * m : 4 * (m + 1)
+                    ],
+                )
+            grouped[("g", i, m)] = gt
 
         def quant(b):
             kind, c, part = b
@@ -175,96 +219,116 @@ def tile_longcatrouter_kernel(tc, hidden_states, weight, out):
 
         acc = {}
 
-        def open_acc(j):
-            acc[j] = psum.tile([P, 512], F32, name="acc%d" % j, tag="acc%d" % j)
+        def open_acc(key, n):
+            acc[key] = psum.tile([P, 512], F32, name="b%d" % n, tag="b%d" % n)
 
-        def drain(j, i, n, on_vector):
+        def drain(key, i, n, on_vector):
             ot = osp.tile([P, n], F32, name="ot%d" % n, tag="ot%d" % n)
             if on_vector:
-                nc.vector.tensor_copy(out=ot[:], in_=acc[j][:, 0:n])
+                nc.vector.tensor_copy(out=ot[:], in_=acc[key][:, 0:n])
             else:
-                nc.scalar.copy(out=ot[:], in_=acc[j][:, 0:n])
+                nc.scalar.copy(out=ot[:], in_=acc[key][:, 0:n])
             e0 = 0 if n == 512 else 512
             nc.sync.dma_start(out=out[P * i : P * (i + 1), e0 : e0 + n], in_=ot[:])
-
-        late = []
 
         def first(g):
             for i in range(4):
                 if g == 0:
-                    open_acc(i)
+                    open_acc(i, 4 + i)
                 mx(acc[i][:], cA, sA, 1024 * g + 512 + P * i, cA, sA, 1024 * g, 512, g)
                 if g == N_PASS - 1:
-                    if i % 2 == 0:
-                        drain(i, i, 512, False)
-                    else:
-                        late.append(i)
+                    drain(i, i, 512, False)
 
-        def token_batch(b):
-            kind, i, part = b
-            if part == 0:
-                open_acc(i - 4)
-            for g in range(4 * part, 4 * part + 4):
-                mx(acc[i - 4][:], cH, sH, 1536 * (i - 4) + P * g, cA, sA, 1024 * g, 512, g)
-            if part == 2:
-                drain(i - 4, i, 512, False)
-
-        def last_low(q):
-            for i in range(4):
-                if q == 0:
-                    open_acc(i)
-                for g in range(4 * q, 4 * q + 4):
-                    mx(acc[i][:, 0:256], cA, sA, 1024 * g + 512 + P * i, cX, sX, 256 * g, 256, g)
-                if q == 2:
-                    drain(i, i, 256, i % 2 == 0)
-
-        def last_high(i):
-            open_acc(i - 4)
+        def token_tile(i, n):
+            open_acc(i, n)
             for g in range(N_PASS):
-                mx(acc[i - 4][:, 0:256], cH, sH, 1536 * (i - 4) + P * g, cX, sX, 256 * g, 256, g)
-            drain(i - 4, i, 256, i % 2 == 0)
+                mx(acc[i][:], cH, sH, 1536 * (i - 4) + P * g, cA, sA, 1024 * g, 512, g)
+            drain(i, i, 512, False)
 
-        runs = [(("w", 0, 0), ("h", 0, 0)), (("w", 0, 1), ("h", 0, 1))]
+        def last(i, n):
+            open_acc(i, n)
+            for g in range(N_PASS):
+                if i < 4:
+                    mx(acc[i][:, 0:256], cA, sA, 1024 * g + 512 + P * i, cX, sX, 256 * g, 256, g)
+                else:
+                    mx(acc[i][:, 0:256], cH, sH, 1536 * (i - 4) + P * g, cX, sX, 256 * g, 256, g)
+            drain(i, i, 256, False)
+
+        rest = [("g", i, part) for i in range(4, 6) for part in range(3)]
+        rest += [("x", half, part) for half in range(2) for part in range(3)]
+
+        steps = [
+            ([("w", 0, 0)], []),
+            ([("h", 0, 0)], []),
+            ([("w", 0, 1)], [0]),
+            ([("h", 0, 1)], []),
+        ]
         for c in range(1, 6):
-            for kind in ("w", "h"):
-                runs.append(((kind, c, 0), (kind, c, 1)))
-        parts = [("g", i, part) for i in range(4, 8) for part in range(3)]
-        parts += [("x", half, part) for half in range(2) for part in range(3)]
-        runs += [(parts[2 * n], parts[2 * n + 1]) for n in range(9)]
+            steps.append(([("w", c, 0), ("w", c, 1)], [2 * c - 2] if c > 1 else [1]))
+            steps.append(([("h", c, 0), ("h", c, 1)], [2 * c - 1] if c > 1 else []))
+        steps.append((rest[0:2], [10]))
+        steps.append((rest[2:5], [11]))
+        steps.append((rest[5:8], [("t", 4)]))
+        steps.append((rest[8:12], [("t", 5)]))
 
-        def multiply(n):
-            if n in (1, 2):
-                first(n - 1)
-            elif 4 <= n <= 13:
-                first(n - 2)
-            elif 14 <= n <= 19:
-                for b in runs[n - 2]:
-                    token_batch(b)
-            elif n == 20:
-                last_low(0)
-                last_low(1)
+        order = [b for batches, mults in steps for b in batches]
+        todo = order[2:]
+        count = 0
 
-        todo = [b for run in runs[1:] for b in run]
-
-        def sort_to(count):
-            while todo and len(sorted_words) < count:
+        def sort_to(n):
+            while todo and len(sorted_words) < n - 2:
                 sort(todo.pop(0))
 
-        for n in range(len(runs)):
-            ahead = 1 if n < 4 else 2
-            one, two = runs[n]
-            transpose_batch(one, 0)
-            transpose_batch(two, 2)
+        previous = None
+        pieces = [(i, r, q) for i in (6, 7) for r in range(4) for q in range(4)]
+        for batches, mults in steps:
+            if ("t", 4) in mults:
+                st["banks"] = 6
+            for b in batches:
+                transpose_batch(b, count < 2)
+                count += 1
+                ahead = 1 if count < 4 else 2 if count < 6 else 3
+                if previous is not None:
+                    quant(previous)
+                sort_to(count + ahead)
+                if count > 25:
+                    for piece in pieces[:3]:
+                        load_turned(*piece)
+                    pieces = pieces[3:]
+                previous = b
+            for m in mults:
+                if isinstance(m, tuple):
+                    token_tile(m[1], 2 + m[1])
+                else:
+                    first(m)
+        quant(previous)
+
+        rows = {}
+
+        def turn(i, n):
+            if n == 0:
+                turned[i] = rawp.tile([P, 3072], F32, name="raw", tag="raw", align_bytes=64)
+            if n < 4:
+                rows[n] = turn_rows(i, n)
             if n > 0:
-                quant(runs[n - 1][1])
-            while late:
-                j = late.pop(0)
-                drain(j, j, 512, True)
-            sort_to(2 * (n + ahead) - 1)
-            quant(one)
-            sort_to(2 * (n + ahead))
-            multiply(n)
-        quant(runs[-1][1])
-        last_low(2)
-        for i in range(4, 8):
-            last_high(i)
+                turn_blocks(i, n - 1, rows[n - 1])
+
+        for n in range(5):
+            turn(6, n)
+        last(0, 6)
+        last(1, 0)
+        for m in range(3):
+            gather_turned(6, m)
+        for n in range(5):
+            if n < 3:
+                quant(("g", 6, n))
+            turn(7, n)
+        for i in range(2, 6):
+            last(i, i - 1)
+        for m in range(3):
+            gather_turned(7, m)
+            quant(("g", 7, m))
+        token_tile(6, 5)
+        last(6, 6)
+        token_tile(7, 7)
+        last(7, 0)

@@ -64,7 +64,7 @@ def tile_longcatrouter_kernel(tc, hidden_states, weight, out):
         loads = []
         for c in range(1, 6):
             loads.extend([("w", c), ("h", c)])
-        loads.extend([("g", 4), ("g", 5), ("x", 0), ("x", 1)])
+        loads.extend([("g", 4), ("g", 5), ("g", 6), ("x", 0), ("x", 1)])
 
         def pump():
             while st["next"] < len(loads):
@@ -254,7 +254,7 @@ def tile_longcatrouter_kernel(tc, hidden_states, weight, out):
                     mx(acc[i][:, 0:256], cH, sH, 1536 * (i - 4) + P * g, cX, sX, 256 * g, 256, g)
             drain(i, i, 256, False)
 
-        rest = [("g", i, part) for i in range(4, 6) for part in range(3)]
+        rest = [("g", i, part) for i in range(4, 7) for part in range(3)]
         rest += [("x", half, part) for half in range(2) for part in range(3)]
 
         steps = [
@@ -269,7 +269,8 @@ def tile_longcatrouter_kernel(tc, hidden_states, weight, out):
         steps.append((rest[0:2], [10]))
         steps.append((rest[2:5], [11]))
         steps.append((rest[5:8], [("t", 4)]))
-        steps.append((rest[8:12], [("t", 5)]))
+        steps.append((rest[8:11], [("t", 5)]))
+        steps.append((rest[11:15], [("t", 6)]))
 
         order = [b for batches, mults in steps for b in batches]
         todo = order[2:]
@@ -280,7 +281,7 @@ def tile_longcatrouter_kernel(tc, hidden_states, weight, out):
                 sort(todo.pop(0))
 
         previous = None
-        pieces = [(i, r, q) for i in (6, 7) for r in range(4) for q in range(4)]
+        pieces = [(i, r, q) for i in (7,) for r in range(4) for q in range(4)]
         for batches, mults in steps:
             if ("t", 4) in mults:
                 st["banks"] = 6
@@ -291,14 +292,14 @@ def tile_longcatrouter_kernel(tc, hidden_states, weight, out):
                 if previous is not None:
                     quant(previous)
                 sort_to(count + ahead)
-                if count > 25:
-                    for piece in pieces[:3]:
+                if count > 28:
+                    for piece in pieces[:2]:
                         load_turned(*piece)
-                    pieces = pieces[3:]
+                    pieces = pieces[2:]
                 previous = b
             for m in mults:
                 if isinstance(m, tuple):
-                    token_tile(m[1], 2 + m[1])
+                    token_tile(m[1], 6 + m[1] % 2)
                 else:
                     first(m)
         quant(previous)
@@ -314,21 +315,13 @@ def tile_longcatrouter_kernel(tc, hidden_states, weight, out):
                 turn_blocks(i, n - 1, rows[n - 1])
 
         for n in range(5):
-            turn(6, n)
-        last(0, 6)
-        last(1, 0)
-        for m in range(3):
-            gather_turned(6, m)
-        for n in range(5):
-            if n < 3:
-                quant(("g", 6, n))
             turn(7, n)
-        for i in range(2, 6):
-            last(i, i - 1)
+        for i in range(3):
+            last(i, (7, 0, 1)[i])
         for m in range(3):
             gather_turned(7, m)
             quant(("g", 7, m))
-        token_tile(6, 5)
-        last(6, 6)
-        token_tile(7, 7)
+        for i in range(3, 7):
+            last(i, i - 1)
+        token_tile(7, 6)
         last(7, 0)

@@ -26,7 +26,7 @@ def tile_longcatrouter_kernel(tc, hidden_states, weight, out):
         headp = ctx.enter_context(tc.tile_pool(name="headp", bufs=1))
         keep = ctx.enter_context(tc.tile_pool(name="keep", bufs=1))
         rawp = ctx.enter_context(tc.tile_pool(name="rawp", bufs=NR))
-        sortp = ctx.enter_context(tc.tile_pool(name="sortp", bufs=6))
+        sortp = ctx.enter_context(tc.tile_pool(name="sortp", bufs=5))
         grp = ctx.enter_context(tc.tile_pool(name="grp", bufs=4))
         osp = ctx.enter_context(tc.tile_pool(name="osp", bufs=4))
         psum = ctx.enter_context(tc.psum_pool(name="psum", bufs=1))
@@ -168,25 +168,22 @@ def tile_longcatrouter_kernel(tc, hidden_states, weight, out):
 
         turned = {}
 
-        def turn_rows(i, r):
-            s = sortp.tile([P, 768], F32, name="sorted", tag="sorted", align_bytes=64)
+        def turn(i, m):
+            s = sortp.tile([P, 1024], F32, name="sorted", tag="sorted", align_bytes=64)
             nc.vector.tensor_copy(
-                out=s[:].rearrange("p (u q) -> p u q", u=2),
-                in_=raw[("v", i)][:].bitcast(F32)[:, 768 * r : 768 * (r + 1)].rearrange("p (q u) -> p u q", u=2),
+                out=s[:].rearrange("p (r u q) -> p r u q", r=4, u=2),
+                in_=raw[("v", i)][:].bitcast(F32).rearrange("p (r m q u) -> p m r u q", r=4, m=3, u=2)[:, m],
             )
-            return s
-
-        def turn_blocks(i, r, s):
-            nc.vector.transpose(turned[i][:, 768 * r : 768 * (r + 1)], s[:])
+            t = sortp.tile([P, 1024], F32, name="sorted", tag="sorted", align_bytes=64)
+            nc.vector.transpose(t[:], s[:])
+            turned[(i, m)] = t
 
         def gather_turned(i, m):
             gt = grp.tile([P, 2048], BF16, name="grouped", tag="grouped", align_bytes=64)
             for r in range(4):
                 nc.scalar.copy(
                     out=gt[:].bitcast(F32).rearrange("p (g r t u) -> p r g t u", g=4, r=4, u=2)[:, r],
-                    in_=turned[i][:, 768 * r : 768 * (r + 1)].rearrange("p (u g t) -> p g t u", u=2, t=32)[
-                        :, 4 * m : 4 * (m + 1)
-                    ],
+                    in_=turned[(i, m)][:, 256 * r : 256 * (r + 1)].rearrange("p (u g t) -> p g t u", u=2, t=32),
                 )
             grouped[("g", i, m)] = gt
 
@@ -223,7 +220,7 @@ def tile_longcatrouter_kernel(tc, hidden_states, weight, out):
             acc[key] = psum.tile([P, 512], F32, name="b%d" % n, tag="b%d" % n)
 
         def drain(key, i, n, on_vector):
-            ot = osp.tile([P, n], F32, name="ot%d" % n, tag="ot%d" % n)
+            ot = osp.tile([P, n], F32, name="ot%d" % n, tag="ot%d" % n, bufs=6 if n == 512 else 4)
             if on_vector:
                 nc.vector.tensor_copy(out=ot[:], in_=acc[key][:, 0:n])
             else:
@@ -292,10 +289,10 @@ def tile_longcatrouter_kernel(tc, hidden_states, weight, out):
                 if previous is not None:
                     quant(previous)
                 sort_to(count + ahead)
-                if count > 28:
-                    for piece in pieces[:2]:
+                if count > 27:
+                    for piece in pieces[:16]:
                         load_turned(*piece)
-                    pieces = pieces[2:]
+                    pieces = []
                 previous = b
             for m in mults:
                 if isinstance(m, tuple):
@@ -304,23 +301,14 @@ def tile_longcatrouter_kernel(tc, hidden_states, weight, out):
                     first(m)
         quant(previous)
 
-        rows = {}
-
-        def turn(i, n):
-            if n == 0:
-                turned[i] = rawp.tile([P, 3072], F32, name="raw", tag="raw", align_bytes=64)
-            if n < 4:
-                rows[n] = turn_rows(i, n)
-            if n > 0:
-                turn_blocks(i, n - 1, rows[n - 1])
-
-        for n in range(5):
-            turn(7, n)
-        for i in range(3):
-            last(i, (7, 0, 1)[i])
+        for m in range(3):
+            turn(7, m)
+        last(0, 7)
+        last(1, 0)
         for m in range(3):
             gather_turned(7, m)
             quant(("g", 7, m))
+        last(2, 1)
         for i in range(3, 7):
             last(i, i - 1)
         token_tile(7, 6)

from contextlib import ExitStack

import concourse.mybir as mybir
from concourse.masks import make_identity

F32 = mybir.dt.float32
BF16 = mybir.dt.bfloat16
U32 = mybir.dt.uint32
U8 = mybir.dt.uint8
FP8X4 = mybir.dt.float8_e4m3fn_x4

P = 128
T_ROWS, D, E = 1024, 6144, 768
N_PASS = 12
FLOPS = 2 * T_ROWS * D * E
NR = 5


def tile_longcatrouter_kernel(tc, hidden_states, weight, out):
    nc = tc.nc
    hid = hidden_states.rearrange("(i p) k -> p i k", p=P)
    wgt = weight.rearrange("(a p) k -> p a k", p=P)

    with ExitStack() as ctx:
        const = ctx.enter_context(tc.tile_pool(name="const", bufs=1))
        headp = ctx.enter_context(tc.tile_pool(name="headp", bufs=1))
        keep = ctx.enter_context(tc.tile_pool(name="keep", bufs=1))
        rawp = ctx.enter_context(tc.tile_pool(name="rawp", bufs=NR))
        sortp = ctx.enter_context(tc.tile_pool(name="sortp", bufs=5))
        grp = ctx.enter_context(tc.tile_pool(name="grp", bufs=4))
        osp = ctx.enter_context(tc.tile_pool(name="osp", bufs=4))
        psum = ctx.enter_context(tc.psum_pool(name="psum", bufs=1))
        ctx.enter_context(tc.manual_schedule())

        raw = {}
        st = {"next": 0, "raw_free": NR, "bank": 0, "banks": 4}

        def new_raw(kind, c):
            width = 4096 if kind in ("w", "h") else 6144
            t = rawp.tile([P, width], BF16, name="raw", tag="raw", align_bytes=64)
            raw[(kind, c)] = t
            return t

        def source(kind, k0, k1):
            if kind == "w":
                return wgt[:, 0:4, k0:k1]
            return hid[:, 0:4, k0:k1]

        def load_first(kind, pl, pairs):
            t = headp.tile([P, 2048], BF16, name="head_%s%d" % (kind, pl), tag="head_%s%d" % (kind, pl))
            raw[(kind, 0, pl)] = t
            src = wgt if kind == "w" else hid
            for a0, a1 in pairs:
                nc.sync.dma_start(
                    out=t[:].rearrange("p (a k) -> p a k", a=4)[:, a0:a1, :],
                    in_=src[:, a0:a1, 512 * pl : 512 * (pl + 1)],
                )

        load_first("w", 0, ((0, 2), (2, 4)))
        load_first("h", 0, ((0, 2), (2, 4)))
        load_first("w", 1, ((0, 4),))
        load_first("h", 1, ((0, 4),))

        loads = []
        for c in range(1, 6):
            loads.extend([("w", c), ("h", c)])
        loads.extend([("g", 4), ("g", 5), ("g", 6), ("x", 0), ("x", 1)])

        def pump():
            while st["next"] < len(loads):
                kind, c = loads[st["next"]]
                if st["raw_free"] == 0:
                    break
                st["raw_free"] -= 1
                st["next"] += 1
                t = new_raw(kind, c)
                if kind == "x":
                    nc.sync.dma_start(
                        out=t[:].rearrange("p (a k) -> p a k", a=2),
                        in_=wgt[:, 4:6, 3072 * c : 3072 * (c + 1)],
                    )
                elif kind == "g":
                    nc.sync.dma_start(out=t[:], in_=hid[:, c, :])
                else:
                    nc.sync.dma_start(
                        out=t[:].rearrange("p (a k) -> p a k", a=4),
                        in_=source(kind, 1024 * c, 1024 * (c + 1)),
                    )

        pump()

        def load_turned(i, r, q):
            if (r, q) == (0, 0):
                new_raw("v", i)
            t0 = P * i + 32 * r
            nc.sync.dma_start(
                out=raw[("v", i)][32 * q : 32 * (q + 1), 1536 * r : 1536 * (r + 1)].rearrange("p (g k) -> p g k", k=P),
                in_=hidden_states[t0 : t0 + 32, :].rearrange("p (g k) -> p g k", k=512)[:, :, P * q : P * (q + 1)],
            )

        ident = const.tile([P, P], F32)
        make_identity(nc, ident[:])

        cA = keep.tile([P, N_PASS * 1024], U32, align_bytes=64)
        sA = keep.tile([P, N_PASS * 1024], U8, align_bytes=64)
        cH = keep.tile([P, N_PASS * 512], U32, align_bytes=64)
        sH = keep.tile([P, N_PASS * 512], U8, align_bytes=64)
        cX = keep.tile([P, N_PASS * 256], U32, align_bytes=64)
        sX = keep.tile([P, N_PASS * 256], U8, align_bytes=64)

        ROWS = {"w": 4, "h": 4, "x": 2, "g": 1}
        PARTS = {"w": 2, "h": 2, "x": 3, "g": 3}
        sorted_words = {}
        grouped = {}

        def batch_words(b):
            kind, c, part = b
            rows = ROWS[kind]
            span = 1024 // rows
            if (kind, c, part) in raw:
                return raw[(kind, c, part)][:].bitcast(F32).rearrange("p (a k) -> p a k", a=rows)
            words = raw[(kind, c)][:].bitcast(F32).rearrange("p (a k) -> p a k", a=rows)
            return words[:, :, span * part : span * (part + 1)]

        def sort(b):
            kind, c, part = b
            rows = ROWS[kind]
            s = sortp.tile([P, 1024], F32, name="sorted", tag="sorted", align_bytes=64)
            nc.vector.tensor_copy(
                out=s[:].rearrange("p (a u q) -> p a u q", a=rows, u=2),
                in_=batch_words(b).rearrange("p a (q u) -> p a u q", u=2),
            )
            sorted_words[b] = s
            if (kind, c) in raw and part == PARTS[kind] - 1:
                st["raw_free"] += 1
                pump()

        def transpose_batch(b, share):
            kind, c, part = b
            rows = ROWS[kind]
            span = 1024 // rows
            gt = grp.tile([P, 2048], BF16, name="grouped", tag="grouped", align_bytes=64)
            for half in range(2):
                n = st["bank"]
                st["bank"] = (n + 1) % st["banks"]
                bk = psum.tile([P, 512], F32, name="b%d" % n, tag="b%d" % n)
                for s in range(2):
                    slot = 2 * half + s
                    a = slot % rows
                    g = slot // rows
                    for u in range(2):
                        if b in sorted_words:
                            k0 = span * a + span // 2 * u + P * g
                            src = sorted_words[b][:, k0 : k0 + P]
                        else:
                            src = batch_words(b)[:, a, 256 * g + u : 256 * (g + 1) : 2]
                        j = 2 * s + u
                        nc.tensor.transpose(bk[:, P * j : P * (j + 1)], src, ident[:])
                dst = gt[:].bitcast(F32)[:, 512 * half : 512 * (half + 1)].rearrange(
                    "p (a r u) -> p a r u", a=2, u=2
                )
                src = bk[:].rearrange("p (a u r) -> p a r u", a=2, u=2)
                if share and half == 1:
                    nc.vector.tensor_copy(out=dst, in_=src)
                else:
                    nc.scalar.copy(out=dst, in_=src)
            grouped[b] = gt

        turned = {}

        def turn(i, m):
            s = sortp.tile([P, 1024], F32, name="sorted", tag="sorted", align_bytes=64)
            nc.vector.tensor_copy(
                out=s[:].rearrange("p (r u q) -> p r u q", r=4, u=2),
                in_=raw[("v", i)][:].bitcast(F32).rearrange("p (r m q u) -> p m r u q", r=4, m=3, u=2)[:, m],
            )
            t = sortp.tile([P, 1024], F32, name="sorted", tag="sorted", align_bytes=64)
            nc.vector.transpose(t[:], s[:])
            turned[(i, m)] = t

        def gather_turned(i, m):
            gt = grp.tile([P, 2048], BF16, name="grouped", tag="grouped", align_bytes=64)
            for r in range(4):
                nc.scalar.copy(
                    out=gt[:].bitcast(F32).rearrange("p (g r t u) -> p r g t u", g=4, r=4, u=2)[:, r],
                    in_=turned[(i, m)][:, 256 * r : 256 * (r + 1)].rearrange("p (u g t) -> p g t u", u=2, t=32),
                )
            grouped[("g", i, m)] = gt

        def quant(b):
            kind, c, part = b
            if kind == "w":
                codes, scales, c0 = cA, sA, 1024 * (2 * c + part)
            elif kind == "h":
                codes, scales, c0 = cA, sA, 1024 * (2 * c + part) + 512
            elif kind == "x":
                codes, scales, c0 = cX, sX, 512 * (3 * c + part)
            else:
                codes, scales, c0 = cH, sH, 1536 * (c - 4) + 512 * part
            nc.vector.quantize_mx(
                out=codes[:, c0 : c0 + 512].bitcast(FP8X4),
                scales=scales[:, c0 : c0 + 512],
                in_=grouped[b][:],
            )

        def mx(acc_ap, lc, ls, l0, rc, rs, r0, n, g):
            nc.tensor.matmul_mx(
                out=acc_ap,
                lhsT=lc[:, l0 : l0 + P].bitcast(FP8X4),
                lhsT_scale=ls[:, l0 : l0 + P],
                rhs=rc[:, r0 : r0 + n].bitcast(FP8X4),
                rhs_scale=rs[:, r0 : r0 + n],
                start=g == 0,
                stop=g == N_PASS - 1,
            )

        acc = {}

        def open_acc(key, n):
            acc[key] = psum.tile([P, 512], F32, name="b%d" % n, tag="b%d" % n)

        def drain(key, i, n, on_vector):
            ot = osp.tile([P, n], F32, name="ot%d" % n, tag="ot%d" % n, bufs=6 if n == 512 else 4)
            if on_vector:
                nc.vector.tensor_copy(out=ot[:], in_=acc[key][:, 0:n])
            else:
                nc.scalar.copy(out=ot[:], in_=acc[key][:, 0:n])
            e0 = 0 if n == 512 else 512
            nc.sync.dma_start(out=out[P * i : P * (i + 1), e0 : e0 + n], in_=ot[:])

        def first(g):
            for i in range(4):
                if g == 0:
                    open_acc(i, 4 + i)
                mx(acc[i][:], cA, sA, 1024 * g + 512 + P * i, cA, sA, 1024 * g, 512, g)
                if g == N_PASS - 1:
                    drain(i, i, 512, False)

        def token_tile(i, n):
            open_acc(i, n)
            for g in range(N_PASS):
                mx(acc[i][:], cH, sH, 1536 * (i - 4) + P * g, cA, sA, 1024 * g, 512, g)
            drain(i, i, 512, False)

        def last(i, n):
            open_acc(i, n)
            for g in range(N_PASS):
                if i < 4:
                    mx(acc[i][:, 0:256], cA, sA, 1024 * g + 512 + P * i, cX, sX, 256 * g, 256, g)
                else:
                    mx(acc[i][:, 0:256], cH, sH, 1536 * (i - 4) + P * g, cX, sX, 256 * g, 256, g)
            drain(i, i, 256, False)

        rest = [("g", i, part) for i in range(4, 7) for part in range(3)]
        rest += [("x", half, part) for half in range(2) for part in range(3)]

        steps = [
            ([("w", 0, 0)], []),
            ([("h", 0, 0)], []),
            ([("w", 0, 1)], [0]),
            ([("h", 0, 1)], []),
        ]
        for c in range(1, 6):
            steps.append(([("w", c, 0), ("w", c, 1)], [2 * c - 2] if c > 1 else [1]))
            steps.append(([("h", c, 0), ("h", c, 1)], [2 * c - 1] if c > 1 else []))
        steps.append((rest[0:2], [10]))
        steps.append((rest[2:5], [11]))
        steps.append((rest[5:8], [("t", 4)]))
        steps.append((rest[8:11], [("t", 5)]))
        steps.append((rest[11:15], [("t", 6)]))

        order = [b for batches, mults in steps for b in batches]
        todo = order[2:]
        count = 0

        def sort_to(n):
            while todo and len(sorted_words) < n - 2:
                sort(todo.pop(0))

        previous = None
        pieces = [(i, r, q) for i in (7,) for r in range(4) for q in range(4)]
        for batches, mults in steps:
            if ("t", 4) in mults:
                st["banks"] = 6
            for b in batches:
                transpose_batch(b, count < 2)
                count += 1
                ahead = 1 if count < 4 else 2 if count < 6 else 3
                if previous is not None:
                    quant(previous)
                sort_to(count + ahead)
                if count > 27:
                    for piece in pieces[:16]:
                        load_turned(*piece)
                    pieces = []
                previous = b
            for m in mults:
                if isinstance(m, tuple):
                    token_tile(m[1], 6 + m[1] % 2)
                else:
                    first(m)
        quant(previous)

        for m in range(3):
            turn(7, m)
        last(0, 7)
        last(1, 0)
        for m in range(3):
            gather_turned(7, m)
            quant(("g", 7, m))
        last(2, 1)
        for i in range(3, 7):
            last(i, i - 1)
        token_tile(7, 6)
        last(7, 0)
